import numpy as np
import ml_dtypes


def mxq(x, axis, fmt="e4m3"):
    dtype, down = {"e4m3": (ml_dtypes.float8_e4m3fn, 7), "e5m2": (ml_dtypes.float8_e5m2, 14)}[fmt]
    v = np.moveaxis(np.asarray(x, np.float32).astype(ml_dtypes.bfloat16).astype(np.float64), axis, -1)
    blocks = v.reshape(v.shape[:-1] + (-1, 32))
    amax = np.abs(blocks).max(-1, keepdims=True)
    byte = np.maximum(np.where(amax > 0, np.frexp(amax)[1] - 1 + 127, 0) - down, 1)
    scale = np.exp2(byte - 127.0)
    codes = (blocks / scale).astype(np.float32).astype(dtype).astype(np.float64)
    return np.moveaxis((codes * scale).reshape(v.shape), -1, axis)


WIDE = False


def mx_kscale(k):
    if not WIDE:
        return np.ones(k)
    levels = np.array([10, -10, 5, -5, 0])
    if k % 512:
        return np.exp2(np.random.permutation(np.resize(levels, k // 32))).repeat(32)
    a = np.empty((k // 512, 16))
    for p in range(k // 512):
        a[p, :8] = np.random.permutation(np.resize(levels, 8))
        for g in range(8):
            far = levels[np.abs(levels - a[p, g]) >= 10]
            a[p, g + 8] = far[np.random.randint(len(far))]
    return np.exp2(a.ravel()).repeat(32)


BF16 = ml_dtypes.bfloat16


def bf(x):
    return np.asarray(x, np.float32).astype(BF16)


def f64(x):
    return np.asarray(x).astype(np.float64)


B, S, K, H, D = 4, 384, 128, 1024, 1024
EPS = 1e-6


def setup_inputs():
    s = mx_kscale(H)
    rows = 0.5 * np.exp(0.5 * np.random.standard_normal((B, S, 1)))
    return {"hidden_states": bf(np.random.standard_normal((B, S, H)) * rows),
            "memory_state": bf(np.random.standard_normal((B, K, H)) * s),
            "q_w": bf(np.random.standard_normal((D, H)) * 1.5 / np.sqrt(H) / s),
            "k_w": bf(np.random.standard_normal((D, H)) * 1.5 / np.sqrt(H) / s),
            "norm_w": bf((1.0 + 0.3 * np.random.standard_normal(H)) * s)}


def reference(hidden_states, memory_state, q_w, k_w, norm_w):
    x = f64(hidden_states)
    normed = x * (1.0 / np.sqrt(np.mean(x * x, axis=-1, keepdims=True) + EPS)) * f64(norm_w)
    pool = np.concatenate([normed, f64(memory_state)], axis=1)
    pq = mxq(pool, 2, "e4m3")
    q = pq[:, :S] @ mxq(f64(q_w), 1, "e4m3").T
    k = pq @ mxq(f64(k_w), 1, "e4m3").T
    return q, k

@@ -1,0 +1,247 @@
+from contextlib import ExitStack
+
+import concourse.masks as masks
+import concourse.mybir as mybir
+
+F32 = mybir.dt.float32
+BF16 = mybir.dt.bfloat16
+I32 = mybir.dt.int32
+U32 = mybir.dt.uint32
+U8 = mybir.dt.uint8
+FP8X4 = mybir.dt.float8_e4m3fn_x4
+ACT = mybir.ActivationFunctionType
+ALU = mybir.AluOpType
+
+P = 128
+PACK = 4
+PAIR = 2
+BATCHES, TOKENS, MEMORY, H, D = 4, 384, 128, 1024, 1024
+EPS = 1e-6
+PASSES = H // (P * PACK)
+HALVES = PACK // PAIR
+BATCH_TILES = TOKENS // P
+TILES = BATCHES * BATCH_TILES
+N_TILE = 512
+ROW_BLOCKS = N_TILE // P
+COLUMN_TILES = D // N_TILE
+SQUARE_AHEAD = 4
+NORM_AHEAD = 3
+TURN_AHEAD = 1
+
+FLOPS = 2 * H * D * BATCHES * (TOKENS + TOKENS + MEMORY)
+
+
+def tile_memresprojections_pa_kernel(
+    tc, hidden_states, memory_state, q_w, k_w, norm_w, out_0, out_1
+):
+    nc = tc.nc
+    with ExitStack() as ctx:
+        ctx.enter_context(tc.manual_schedule())
+        const = ctx.enter_context(tc.tile_pool(name="const", bufs=1))
+        inputs = ctx.enter_context(tc.tile_pool(name="inputs", bufs=1))
+        operands = ctx.enter_context(tc.tile_pool(name="operands", bufs=1))
+        stage = ctx.enter_context(tc.tile_pool(name="stage", bufs=4))
+        results = ctx.enter_context(tc.tile_pool(name="results", bufs=8))
+        banks = ctx.enter_context(tc.psum_pool(name="banks", bufs=8))
+
+        gain_row = const.tile([P, H], BF16)
+        nc.vector.memset(gain_row[:].bitcast(I32), 0)
+        nc.sync.dma_start(out=gain_row[0:1, :], in_=norm_w.unsqueeze(0))
+
+        token_rows = hidden_states.flatten_outer_dims()
+        tokens = {}
+
+        def load_tokens(n):
+            tokens[n] = inputs.tile([P, H], BF16, name="tokens%d" % n)
+            nc.sync.dma_start(out=tokens[n][:], in_=token_rows[n * P : (n + 1) * P, :])
+
+        def load_rows(source, label):
+            rows = inputs.tile([P, ROW_BLOCKS, H], BF16, name=label)
+            nc.sync.dma_start(out=rows[:], in_=source.rearrange("(j p) h -> p j h", p=P))
+            return rows
+
+        for n in range(NORM_AHEAD):
+            load_tokens(n)
+        q_rows0 = load_rows(q_w[0:N_TILE, :], "q_rows0")
+        q_rows1 = load_rows(q_w[N_TILE:D, :], "q_rows1")
+        k_rows0 = load_rows(k_w[0:N_TILE, :], "k_rows0")
+        k_rows1 = load_rows(k_w[N_TILE:D, :], "k_rows1")
+        load_tokens(NORM_AHEAD)
+        memory_rows = load_rows(memory_state.flatten_outer_dims(), "memory_rows")
+        for n in range(NORM_AHEAD + 1, TILES):
+            load_tokens(n)
+
+        minus_half = const.tile([P, 1], F32)
+        nc.vector.memset(minus_half[:], -0.5)
+        table_warmer = const.tile([P, 1], F32)
+        nc.scalar.activation(out=table_warmer[:], in_=minus_half[:], func=ACT.Square)
+        ones = const.tile([P, P], BF16)
+        nc.vector.memset(ones[:], 1.0)
+        ident_f32 = const.tile([P, P], F32)
+        masks.make_identity(nc, ident_f32[:])
+        ident_bf16 = const.tile([P, P], BF16)
+        masks.make_identity(nc, ident_bf16[:])
+
+        gain = const.tile([P, PACK, H // PACK], BF16)
+        words = N_TILE // PACK
+        for c in range(H // N_TILE):
+            spread = banks.tile([P, N_TILE], F32, tag="bank")
+            nc.tensor.matmul(
+                spread[:], lhsT=ones[:], rhs=gain_row[:, c * N_TILE : (c + 1) * N_TILE],
+                start=True, stop=True,
+            )
+            nc.vector.tensor_copy(
+                out=gain[:, :, c * words : (c + 1) * words],
+                in_=spread[:].rearrange("p (w t) -> p t w", t=PACK),
+            )
+
+        inv_rms = {}
+        normed = {}
+        turned = {}
+        grouped = {}
+        pool_mx = {}
+
+        def mean_square(n):
+            squares = stage.tile([P, H], BF16, tag="squares")
+            mean_sq = stage.tile([P, 1], F32, tag="mean_sq")
+            nc.scalar.activation(
+                out=squares[:], in_=tokens[n][:], func=ACT.Square, scale=H**-0.5, accum_out=mean_sq[:]
+            )
+            shifted = stage.tile([P, 1], F32, tag="shifted")
+            nc.gpsimd.tensor_scalar(
+                out=shifted[:], in0=mean_sq[:], scalar1=1.0, scalar2=EPS, op0=ALU.mult, op1=ALU.add
+            )
+            inv_rms[n] = stage.tile([P, 1], F32, tag="inv_rms", name="inv_rms%d" % n)
+            nc.gpsimd.tensor_tensor(out=inv_rms[n][:], in0=shifted[:], in1=minus_half[:], op=ALU.pow)
+
+        def norm(n):
+            normed[n] = stage.tile([P, PACK, H // PACK], BF16, tag="normed", name="normed%d" % n)
+            nc.vector.scalar_tensor_tensor(
+                out=normed[n][:],
+                in0=tokens[n][:].rearrange("p (w t) -> p t w", t=PACK),
+                scalar=inv_rms[n][:],
+                in1=gain[:],
+                op0=ALU.mult,
+                op1=ALU.mult,
+            )
+
+        def turn(n):
+            turned[n] = banks.tile([P, PASSES, PACK, P], BF16, tag="bank", name="turned%d" % n)
+            for g in range(PASSES):
+                for t in range(PACK):
+                    nc.tensor.transpose(
+                        turned[n][:, g, t, :], normed[n][:, t, g * P : (g + 1) * P], ident_bf16[:]
+                    )
+
+        def group(n):
+            grouped[n] = stage.tile(
+                [P, PASSES, P, PACK], BF16, tag="grouped", name="grouped%d" % n, align_bytes=64
+            )
+            nc.scalar.copy(out=grouped[n][:], in_=turned[n][:].rearrange("p g t r -> p g r t"))
+
+        def quantise(n):
+            codes = operands.tile([P, PASSES, P], U32, name="codes%d" % n, align_bytes=64)
+            scales = operands.tile([P, PASSES, P], U8, name="scales%d" % n, align_bytes=64)
+            nc.vector.quantize_mx(
+                out=codes[:].rearrange("p g r -> p (g r)").bitcast(FP8X4),
+                scales=scales[:].rearrange("p g r -> p (g r)"),
+                in_=grouped[n][:].rearrange("p g r t -> p (g r t)"),
+            )
+            pool_mx[n] = (codes, scales)
+
+        def matmuls(token_mx, token_columns, weight_mx):
+            token_codes, token_scales = token_mx
+            sums = []
+            for weight_codes, weight_scales in weight_mx:
+                bank = banks.tile([P, N_TILE], F32, tag="bank")
+                for g in range(PASSES):
+                    nc.tensor.matmul_mx(
+                        out=bank[:],
+                        lhsT=token_codes[:, g, token_columns].bitcast(FP8X4),
+                        lhsT_scale=token_scales[:, g, token_columns],
+                        rhs=weight_codes[:, g, :].bitcast(FP8X4),
+                        rhs_scale=weight_scales[:, g, :],
+                        start=(g == 0),
+                        stop=(g == PASSES - 1),
+                    )
+                sums.append(bank)
+            return sums
+
+        def store(sums, copies, out_rows):
+            result = results.tile([P, D], F32, tag="result")
+            for c in range(COLUMN_TILES):
+                copies[c](out=result[:, c * N_TILE : (c + 1) * N_TILE], in_=sums[c][:])
+            nc.sync.dma_start(out=out_rows, in_=result[:])
+
+        def quantise_rows(rows, label):
+            side_by_side = stage.tile(
+                [P, PASSES * N_TILE * PACK], BF16, tag="side_by_side", bufs=2, align_bytes=64
+            )
+            as_words = side_by_side[:].bitcast(F32).rearrange("p (g r u) -> p g r u", g=PASSES, u=HALVES)
+            row_banks = []
+            for j in range(ROW_BLOCKS):
+                words = rows[:, j, :].bitcast(F32)
+                bank = banks.tile([P, PASSES, HALVES, P], F32, tag="bank")
+                for g in range(PASSES):
+                    for u in range(HALVES):
+                        first = HALVES * P * g
+                        nc.tensor.transpose(
+                            bank[:, g, u, :], words[:, first + u : first + HALVES * P : HALVES], ident_f32[:]
+                        )
+                row_banks.append(bank)
+            for j in range(ROW_BLOCKS):
+                copy = nc.vector.tensor_copy if j == 0 else nc.scalar.copy
+                copy(
+                    out=as_words[:, :, j * P : (j + 1) * P, :],
+                    in_=row_banks[j][:].rearrange("p g u r -> p g r u"),
+                )
+            codes = operands.tile([P, PASSES, N_TILE], U32, name=label + "_codes", align_bytes=64)
+            scales = operands.tile([P, PASSES, N_TILE], U8, name=label + "_scales", align_bytes=64)
+            width = N_TILE * PACK
+            for g in range(PASSES):
+                nc.vector.quantize_mx(
+                    out=codes[:, g, :].bitcast(FP8X4),
+                    scales=scales[:, g, :],
+                    in_=side_by_side[:, g * width : (g + 1) * width],
+                )
+            return codes, scales
+
+        for n in range(NORM_AHEAD):
+            mean_square(n)
+            norm(n)
+        for n in range(TURN_AHEAD):
+            turn(n)
+            group(n)
+            quantise(n)
+        q_mx = [quantise_rows(q_rows0, "q0"), quantise_rows(q_rows1, "q1")]
+        k_mx = [quantise_rows(k_rows0, "k0"), quantise_rows(k_rows1, "k1")]
+        for n in range(NORM_AHEAD, SQUARE_AHEAD):
+            mean_square(n)
+
+        q_copies = [nc.scalar.copy, nc.vector.tensor_copy]
+        k_copies = [nc.vector.tensor_copy, nc.vector.tensor_copy]
+        memory_copies = [nc.scalar.copy, nc.scalar.copy]
+
+        q_out = out_0.flatten_outer_dims()
+        all_columns = slice(0, P)
+        for n in range(TILES):
+            b, i = divmod(n, BATCH_TILES)
+            if n + TURN_AHEAD < TILES:
+                turn(n + TURN_AHEAD)
+            q_sums = matmuls(pool_mx[n], all_columns, q_mx)
+            k_sums = matmuls(pool_mx[n], all_columns, k_mx)
+            if n + TURN_AHEAD < TILES:
+                group(n + TURN_AHEAD)
+            store(q_sums, q_copies, q_out[n * P : (n + 1) * P, :])
+            if n + TURN_AHEAD < TILES:
+                quantise(n + TURN_AHEAD)
+            store(k_sums, k_copies, out_1[b, i * P : (i + 1) * P, :])
+            if n + SQUARE_AHEAD < TILES:
+                mean_square(n + SQUARE_AHEAD)
+            if n + NORM_AHEAD < TILES:
+                norm(n + NORM_AHEAD)
+            if n == 0:
+                memory_mx = quantise_rows(memory_rows, "memory")
+            if i == BATCH_TILES - 1:
+                memory_sums = matmuls(memory_mx, slice(b * P, (b + 1) * P), k_mx)
+                store(memory_sums, memory_copies, out_1[b, TOKENS : TOKENS + MEMORY, :])

@@ -24,9 +24,7 @@ TILES = BATCHES * BATCH_TILES
 N_TILE = 512
 ROW_BLOCKS = N_TILE // P
 COLUMN_TILES = D // N_TILE
-SQUARE_AHEAD = 4
-NORM_AHEAD = 3
-TURN_AHEAD = 1
+CHUNKS = 2 * COLUMN_TILES
 
 FLOPS = 2 * H * D * BATCHES * (TOKENS + TOKENS + MEMORY)
 
@@ -41,12 +39,11 @@ def tile_memresprojections_pa_kernel(
         inputs = ctx.enter_context(tc.tile_pool(name="inputs", bufs=1))
         operands = ctx.enter_context(tc.tile_pool(name="operands", bufs=1))
         stage = ctx.enter_context(tc.tile_pool(name="stage", bufs=4))
-        results = ctx.enter_context(tc.tile_pool(name="results", bufs=8))
+        results = ctx.enter_context(tc.tile_pool(name="results", bufs=14))
         banks = ctx.enter_context(tc.psum_pool(name="banks", bufs=8))
 
         gain_row = const.tile([P, H], BF16)
         nc.vector.memset(gain_row[:].bitcast(I32), 0)
-        nc.sync.dma_start(out=gain_row[0:1, :], in_=norm_w.unsqueeze(0))
 
         token_rows = hidden_states.flatten_outer_dims()
         tokens = {}
@@ -55,20 +52,28 @@ def tile_memresprojections_pa_kernel(
             tokens[n] = inputs.tile([P, H], BF16, name="tokens%d" % n)
             nc.sync.dma_start(out=tokens[n][:], in_=token_rows[n * P : (n + 1) * P, :])
 
-        def load_rows(source, label):
-            rows = inputs.tile([P, ROW_BLOCKS, H], BF16, name=label)
-            nc.sync.dma_start(out=rows[:], in_=source.rearrange("(j p) h -> p j h", p=P))
-            return rows
+        chunk_rows = {}
 
-        for n in range(NORM_AHEAD):
-            load_tokens(n)
-        q_rows0 = load_rows(q_w[0:N_TILE, :], "q_rows0")
-        q_rows1 = load_rows(q_w[N_TILE:D, :], "q_rows1")
-        k_rows0 = load_rows(k_w[0:N_TILE, :], "k_rows0")
-        k_rows1 = load_rows(k_w[N_TILE:D, :], "k_rows1")
-        load_tokens(NORM_AHEAD)
-        memory_rows = load_rows(memory_state.flatten_outer_dims(), "memory_rows")
-        for n in range(NORM_AHEAD + 1, TILES):
+        def load_chunk(c, source, pieces):
+            chunk_rows[c] = inputs.tile([P, ROW_BLOCKS, H], BF16, name="rows%d" % c)
+            blocks = source.rearrange("(j p) h -> p j h", p=P)
+            step = ROW_BLOCKS // pieces
+            for j in range(0, ROW_BLOCKS, step):
+                nc.sync.dma_start(out=chunk_rows[c][:, j : j + step, :], in_=blocks[:, j : j + step, :])
+
+        load_tokens(0)
+        nc.sync.dma_start(out=gain_row[0:1, :], in_=norm_w.unsqueeze(0))
+        load_chunk(0, q_w[0:N_TILE, :], 4)
+        load_tokens(1)
+        load_chunk(1, q_w[N_TILE:D, :], 2)
+        load_tokens(2)
+        load_chunk(2, k_w[0:N_TILE, :], 2)
+        load_tokens(3)
+        load_chunk(3, k_w[N_TILE:D, :], 2)
+        load_tokens(4)
+        load_tokens(5)
+        load_chunk(CHUNKS, memory_state.flatten_outer_dims(), 2)
+        for n in range(6, TILES):
             load_tokens(n)
 
         minus_half = const.tile([P, 1], F32)
@@ -77,12 +82,10 @@ def tile_memresprojections_pa_kernel(
         nc.scalar.activation(out=table_warmer[:], in_=minus_half[:], func=ACT.Square)
         ones = const.tile([P, P], BF16)
         nc.vector.memset(ones[:], 1.0)
-        ident_f32 = const.tile([P, P], F32)
-        masks.make_identity(nc, ident_f32[:])
-        ident_bf16 = const.tile([P, P], BF16)
-        masks.make_identity(nc, ident_bf16[:])
+        ident = const.tile([P, P], F32)
+        masks.make_identity(nc, ident[:])
 
-        gain = const.tile([P, PACK, H // PACK], BF16)
+        gain = const.tile([P, HALVES, H // PACK, PAIR], BF16)
         words = N_TILE // PACK
         for c in range(H // N_TILE):
             spread = banks.tile([P, N_TILE], F32, tag="bank")
@@ -91,8 +94,8 @@ def tile_memresprojections_pa_kernel(
                 start=True, stop=True,
             )
             nc.vector.tensor_copy(
-                out=gain[:, :, c * words : (c + 1) * words],
-                in_=spread[:].rearrange("p (w t) -> p t w", t=PACK),
+                out=gain[:, :, c * words : (c + 1) * words, :],
+                in_=spread[:].rearrange("p (w u e) -> p u w e", u=HALVES, e=PAIR),
             )
 
         inv_rms = {}
@@ -102,7 +105,7 @@ def tile_memresprojections_pa_kernel(
         pool_mx = {}
 
         def mean_square(n):
-            squares = stage.tile([P, H], BF16, tag="squares")
+            squares = stage.tile([P, H], BF16, tag="squares", bufs=2)
             mean_sq = stage.tile([P, 1], F32, tag="mean_sq")
             nc.scalar.activation(
                 out=squares[:], in_=tokens[n][:], func=ACT.Square, scale=H**-0.5, accum_out=mean_sq[:]
@@ -115,133 +118,191 @@ def tile_memresprojections_pa_kernel(
             nc.gpsimd.tensor_tensor(out=inv_rms[n][:], in0=shifted[:], in1=minus_half[:], op=ALU.pow)
 
         def norm(n):
-            normed[n] = stage.tile([P, PACK, H // PACK], BF16, tag="normed", name="normed%d" % n)
-            nc.vector.scalar_tensor_tensor(
-                out=normed[n][:],
-                in0=tokens[n][:].rearrange("p (w t) -> p t w", t=PACK),
-                scalar=inv_rms[n][:],
-                in1=gain[:],
-                op0=ALU.mult,
-                op1=ALU.mult,
-            )
+            normed[n] = stage.tile([P, HALVES, H // PACK, PAIR], BF16, tag="normed", name="normed%d" % n)
+            by_half = tokens[n][:].rearrange("p (w u e) -> p u w e", u=HALVES, e=PAIR)
+            for u in range(HALVES):
+                nc.vector.scalar_tensor_tensor(
+                    out=normed[n][:, u, :, :],
+                    in0=by_half[:, u, :, :],
+                    scalar=inv_rms[n][:],
+                    in1=gain[:, u, :, :],
+                    op0=ALU.mult,
+                    op1=ALU.mult,
+                )
 
         def turn(n):
-            turned[n] = banks.tile([P, PASSES, PACK, P], BF16, tag="bank", name="turned%d" % n)
+            turned[n] = banks.tile([P, PASSES, HALVES, P], F32, tag="bank", name="turned%d" % n)
+            pairs = normed[n][:].rearrange("p u w e -> p (u w e)").bitcast(F32)
             for g in range(PASSES):
-                for t in range(PACK):
-                    nc.tensor.transpose(
-                        turned[n][:, g, t, :], normed[n][:, t, g * P : (g + 1) * P], ident_bf16[:]
-                    )
+                for u in range(HALVES):
+                    first = (PASSES * u + g) * P
+                    nc.tensor.transpose(turned[n][:, g, u, :], pairs[:, first : first + P], ident[:])
 
         def group(n):
             grouped[n] = stage.tile(
-                [P, PASSES, P, PACK], BF16, tag="grouped", name="grouped%d" % n, align_bytes=64
+                [P, PASSES * P * PACK], BF16, tag="grouped", name="grouped%s" % str(n), align_bytes=64
             )
-            nc.scalar.copy(out=grouped[n][:], in_=turned[n][:].rearrange("p g t r -> p g r t"))
+            nc.scalar.copy(
+                out=grouped[n][:].bitcast(F32).rearrange("p (g r u) -> p g r u", g=PASSES, u=HALVES),
+                in_=turned[n][:].rearrange("p g u r -> p g r u"),
+            )
 
         def quantise(n):
-            codes = operands.tile([P, PASSES, P], U32, name="codes%d" % n, align_bytes=64)
-            scales = operands.tile([P, PASSES, P], U8, name="scales%d" % n, align_bytes=64)
+            codes = operands.tile([P, PASSES, P], U32, name="codes%s" % str(n), align_bytes=64)
+            scales = operands.tile([P, PASSES, P], U8, name="scales%s" % str(n), align_bytes=64)
             nc.vector.quantize_mx(
                 out=codes[:].rearrange("p g r -> p (g r)").bitcast(FP8X4),
                 scales=scales[:].rearrange("p g r -> p (g r)"),
-                in_=grouped[n][:].rearrange("p g r t -> p (g r t)"),
+                in_=grouped[n][:],
             )
             pool_mx[n] = (codes, scales)
 
-        def matmuls(token_mx, token_columns, weight_mx):
-            token_codes, token_scales = token_mx
-            sums = []
-            for weight_codes, weight_scales in weight_mx:
-                bank = banks.tile([P, N_TILE], F32, tag="bank")
-                for g in range(PASSES):
-                    nc.tensor.matmul_mx(
-                        out=bank[:],
-                        lhsT=token_codes[:, g, token_columns].bitcast(FP8X4),
-                        lhsT_scale=token_scales[:, g, token_columns],
-                        rhs=weight_codes[:, g, :].bitcast(FP8X4),
-                        rhs_scale=weight_scales[:, g, :],
-                        start=(g == 0),
-                        stop=(g == PASSES - 1),
-                    )
-                sums.append(bank)
-            return sums
 
-        def store(sums, copies, out_rows):
-            result = results.tile([P, D], F32, tag="result")
-            for c in range(COLUMN_TILES):
-                copies[c](out=result[:, c * N_TILE : (c + 1) * N_TILE], in_=sums[c][:])
-            nc.sync.dma_start(out=out_rows, in_=result[:])
+        def turn_memory(b):
+            key = ("m", b)
+            turned[key] = banks.tile([P, PASSES, HALVES, P], F32, tag="bank", name="mturned%d" % b)
+            pairs = chunk_rows[CHUNKS][:, b, :].bitcast(F32)
+            for g in range(PASSES):
+                for u in range(HALVES):
+                    first = HALVES * P * g + u
+                    nc.tensor.transpose(turned[key][:, g, u, :], pairs[:, first : HALVES * P * (g + 1) : HALVES], ident[:])
 
-        def quantise_rows(rows, label):
-            side_by_side = stage.tile(
-                [P, PASSES * N_TILE * PACK], BF16, tag="side_by_side", bufs=2, align_bytes=64
+        side_by_side = {}
+        chunk_mx = {}
+
+        def turn_chunk(c):
+            side_by_side[c] = stage.tile(
+                [P, PASSES * N_TILE * PACK], BF16, tag="side", name="side%d" % c, bufs=2, align_bytes=64
             )
-            as_words = side_by_side[:].bitcast(F32).rearrange("p (g r u) -> p g r u", g=PASSES, u=HALVES)
-            row_banks = []
+            as_pairs = side_by_side[c][:].bitcast(F32).rearrange("p (g r u) -> p g r u", g=PASSES, u=HALVES)
             for j in range(ROW_BLOCKS):
-                words = rows[:, j, :].bitcast(F32)
+                pairs = chunk_rows[c][:, j, :].bitcast(F32)
                 bank = banks.tile([P, PASSES, HALVES, P], F32, tag="bank")
                 for g in range(PASSES):
                     for u in range(HALVES):
-                        first = HALVES * P * g
+                        first = HALVES * P * g + u
                         nc.tensor.transpose(
-                            bank[:, g, u, :], words[:, first + u : first + HALVES * P : HALVES], ident_f32[:]
+                            bank[:, g, u, :], pairs[:, first : HALVES * P * (g + 1) : HALVES], ident[:]
                         )
-                row_banks.append(bank)
-            for j in range(ROW_BLOCKS):
                 copy = nc.vector.tensor_copy if j == 0 else nc.scalar.copy
                 copy(
-                    out=as_words[:, :, j * P : (j + 1) * P, :],
-                    in_=row_banks[j][:].rearrange("p g u r -> p g r u"),
+                    out=as_pairs[:, :, j * P : (j + 1) * P, :],
+                    in_=bank[:].rearrange("p g u r -> p g r u"),
                 )
-            codes = operands.tile([P, PASSES, N_TILE], U32, name=label + "_codes", align_bytes=64)
-            scales = operands.tile([P, PASSES, N_TILE], U8, name=label + "_scales", align_bytes=64)
+
+        def quantise_chunk(c):
+            codes = operands.tile([P, PASSES, N_TILE], U32, name="chunk_codes%d" % c, align_bytes=64)
+            scales = operands.tile([P, PASSES, N_TILE], U8, name="chunk_scales%d" % c, align_bytes=64)
             width = N_TILE * PACK
             for g in range(PASSES):
                 nc.vector.quantize_mx(
                     out=codes[:, g, :].bitcast(FP8X4),
                     scales=scales[:, g, :],
-                    in_=side_by_side[:, g * width : (g + 1) * width],
+                    in_=side_by_side[c][:, g * width : (g + 1) * width],
                 )
-            return codes, scales
-
-        for n in range(NORM_AHEAD):
-            mean_square(n)
-            norm(n)
-        for n in range(TURN_AHEAD):
-            turn(n)
-            group(n)
-            quantise(n)
-        q_mx = [quantise_rows(q_rows0, "q0"), quantise_rows(q_rows1, "q1")]
-        k_mx = [quantise_rows(k_rows0, "k0"), quantise_rows(k_rows1, "k1")]
-        for n in range(NORM_AHEAD, SQUARE_AHEAD):
-            mean_square(n)
-
-        q_copies = [nc.scalar.copy, nc.vector.tensor_copy]
-        k_copies = [nc.vector.tensor_copy, nc.vector.tensor_copy]
-        memory_copies = [nc.scalar.copy, nc.scalar.copy]
+            chunk_mx[c] = (codes, scales)
 
         q_out = out_0.flatten_outer_dims()
-        all_columns = slice(0, P)
-        for n in range(TILES):
+        result_tiles = {}
+
+        def multiply(token_mx, token_columns, c):
+            token_codes, token_scales = token_mx
+            chunk_codes, chunk_scales = chunk_mx[c]
+            bank = banks.tile([P, N_TILE], F32, tag="bank")
+            for g in range(PASSES):
+                nc.tensor.matmul_mx(
+                    out=bank[:],
+                    lhsT=token_codes[:, g, token_columns].bitcast(FP8X4),
+                    lhsT_scale=token_scales[:, g, token_columns],
+                    rhs=chunk_codes[:, g, :].bitcast(FP8X4),
+                    rhs_scale=chunk_scales[:, g, :],
+                    start=(g == 0),
+                    stop=(g == PASSES - 1),
+                )
+            return bank
+
+        def empty(bank, key, out_rows, c):
+            column = c % COLUMN_TILES
+            if column == 0:
+                result_tiles[key] = results.tile([P, D], F32, tag="result", name="result_%s%d" % key)
+            result = result_tiles[key]
+            copy = nc.scalar.copy if column == 0 else nc.vector.tensor_copy
+            copy(out=result[:, column * N_TILE : (column + 1) * N_TILE], in_=bank[:])
+            if column == COLUMN_TILES - 1:
+                nc.sync.dma_start(out=out_rows, in_=result[:])
+
+        def token_product(n, c):
             b, i = divmod(n, BATCH_TILES)
-            if n + TURN_AHEAD < TILES:
-                turn(n + TURN_AHEAD)
-            q_sums = matmuls(pool_mx[n], all_columns, q_mx)
-            k_sums = matmuls(pool_mx[n], all_columns, k_mx)
-            if n + TURN_AHEAD < TILES:
-                group(n + TURN_AHEAD)
-            store(q_sums, q_copies, q_out[n * P : (n + 1) * P, :])
-            if n + TURN_AHEAD < TILES:
-                quantise(n + TURN_AHEAD)
-            store(k_sums, k_copies, out_1[b, i * P : (i + 1) * P, :])
-            if n + SQUARE_AHEAD < TILES:
-                mean_square(n + SQUARE_AHEAD)
-            if n + NORM_AHEAD < TILES:
-                norm(n + NORM_AHEAD)
-            if n == 0:
-                memory_mx = quantise_rows(memory_rows, "memory")
-            if i == BATCH_TILES - 1:
-                memory_sums = matmuls(memory_mx, slice(b * P, (b + 1) * P), k_mx)
-                store(memory_sums, memory_copies, out_1[b, TOKENS : TOKENS + MEMORY, :])
+            bank = multiply(pool_mx[n], slice(0, P), c)
+            if c < COLUMN_TILES:
+                return bank, ("q", n), q_out[n * P : (n + 1) * P, :], c
+            return bank, ("k", n), out_1[b, i * P : (i + 1) * P, :], c
+
+        def memory_product(b, c):
+            bank = multiply(pool_mx[("m", b)], slice(0, P), c)
+            return bank, ("m", b), out_1[b, TOKENS : TOKENS + MEMORY, :], c
+
+        def became_possible(w):
+            return [(n, c) for c in range(w + 1) for n in range(w + 1) if max(n, c) == w]
+
+        mean_square(0)
+        norm(0)
+        turn_chunk(0)
+        turn(0)
+        group(0)
+        mean_square(1)
+        quantise_chunk(0)
+        quantise(0)
+        norm(1)
+        for w in range(1, CHUNKS):
+            turn_chunk(w)
+            sums = [token_product(n, c) for n, c in became_possible(w - 1)]
+            turn(w)
+            mean_square(w + 1)
+            for s in sums[:len(sums)//2]:
+                empty(*s)
+            quantise_chunk(w)
+            for s in sums[len(sums)//2:]:
+                empty(*s)
+            group(w)
+            quantise(w)
+            norm(w + 1)
+        turn_memory(0)
+        turn(CHUNKS)
+        mean_square(CHUNKS + 1)
+        group(("m", 0))
+        quantise(("m", 0))
+        sums = [token_product(n, c) for n, c in became_possible(CHUNKS - 1)]
+        group(CHUNKS)
+        for s in sums[:3]:
+            empty(*s)
+        quantise(CHUNKS)
+        norm(CHUNKS + 1)
+        for s in sums[3:]:
+            empty(*s)
+        mean_square(CHUNKS + 2)
+        for n in range(CHUNKS + 1, TILES + 1):
+            b, odd = divmod(n - CHUNKS - 1, 2)
+            if n + 2 < TILES:
+                mean_square(n + 2)
+            if n < TILES:
+                turn(n)
+            if odd and b < 3:
+                turn_memory(b + 1)
+            sums = [token_product(n - 1, c) for c in range(CHUNKS)]
+            if not odd and b < 4:
+                sums += [memory_product(b, c) for c in range(COLUMN_TILES, CHUNKS)]
+            if n + 1 < TILES:
+                norm(n + 1)
+            if n < TILES:
+                group(n)
+            if odd and b < 3:
+                group(("m", b + 1))
+            for s in sums[:2]:
+                empty(*s)
+            if n < TILES:
+                quantise(n)
+            if odd and b < 3:
+                quantise(("m", b + 1))
+            for s in sums[2:]:
+                empty(*s)

@@ -245,64 +245,75 @@ def tile_memresprojections_pa_kernel(
         def became_possible(w):
             return [(n, c) for c in range(w + 1) for n in range(w + 1) if max(n, c) == w]
 
+        def products(pairs):
+            return [token_product(n, c) for n, c in pairs]
+
+        def empty_all(sums):
+            for s in sums:
+                empty(*s)
+
         mean_square(0)
         norm(0)
         turn_chunk(0)
         turn(0)
-        group(0)
         mean_square(1)
+        group(0)
+        turn_chunk(1)
+        norm(1)
+        turn(1)
         quantise_chunk(0)
         quantise(0)
-        norm(1)
-        for w in range(1, CHUNKS):
-            turn_chunk(w)
-            sums = [token_product(n, c) for n, c in became_possible(w - 1)]
-            turn(w)
-            mean_square(w + 1)
-            for s in sums[:len(sums)//2]:
-                empty(*s)
-            quantise_chunk(w)
-            for s in sums[len(sums)//2:]:
-                empty(*s)
-            group(w)
-            quantise(w)
-            norm(w + 1)
+        mean_square(2)
+        sums = products([(0, 0)])
+        group(1)
+        norm(2)
+        quantise(1)
+        quantise_chunk(1)
+        empty_all(sums)
+        mean_square(3)
+        turn_chunk(2)
+        turn(2)
+        sums = products([(1, 0), (0, 1), (1, 1)])
+        norm(3)
+        group(2)
+        quantise_chunk(2)
+        quantise(2)
+        empty_all(sums)
+        mean_square(4)
+        turn_chunk(3)
         turn_memory(0)
-        turn(CHUNKS)
-        mean_square(CHUNKS + 1)
+        mean_square(5)
+        norm(4)
+        quantise_chunk(3)
         group(("m", 0))
+        sums = products([(2, 0), (2, 1), (0, 2), (1, 2), (2, 2)])
+        empty_all(sums[:2])
+        norm(5)
         quantise(("m", 0))
-        sums = [token_product(n, c) for n, c in became_possible(CHUNKS - 1)]
-        group(CHUNKS)
-        for s in sums[:3]:
-            empty(*s)
-        quantise(CHUNKS)
-        norm(CHUNKS + 1)
-        for s in sums[3:]:
-            empty(*s)
-        mean_square(CHUNKS + 2)
-        for n in range(CHUNKS + 1, TILES + 1):
-            b, odd = divmod(n - CHUNKS - 1, 2)
-            if n + 2 < TILES:
-                mean_square(n + 2)
-            if n < TILES:
+        empty_all(sums[2:])
+        sums = products([(0, 3), (1, 3), (2, 3)])
+        empty_all(sums)
+        mean_square(6)
+        for b in range(1, BATCHES):
+            t = [BATCH_TILES * b + i for i in range(BATCH_TILES)]
+            m = ("m", b)
+            u = [n + BATCH_TILES for n in t if n + BATCH_TILES < TILES]
+            for n in t:
                 turn(n)
-            if odd and b < 3:
-                turn_memory(b + 1)
-            sums = [token_product(n - 1, c) for c in range(CHUNKS)]
-            if not odd and b < 4:
-                sums += [memory_product(b, c) for c in range(COLUMN_TILES, CHUNKS)]
-            if n + 1 < TILES:
-                norm(n + 1)
-            if n < TILES:
-                group(n)
-            if odd and b < 3:
-                group(("m", b + 1))
-            for s in sums[:2]:
-                empty(*s)
-            if n < TILES:
-                quantise(n)
-            if odd and b < 3:
-                quantise(("m", b + 1))
-            for s in sums[2:]:
+            turn_memory(b)
+            group(t[0])
+            quantise(t[0])
+            group(t[1])
+            work = [(memory_product, b - 1, 2), (memory_product, b - 1, 3)]
+            for n in t:
+                work += [(token_product, n, c) for c in range(CHUNKS)]
+            if b == BATCHES - 1:
+                work[-CHUNKS:-CHUNKS] = [(memory_product, b, 2), (memory_product, b, 3)]
+            jobs = [[(quantise, t[1]), (group, t[2])], [(quantise, t[2]), (group, m)], [(quantise, m)]]
+            jobs += [[(mean_square, u[1])], [(norm, u[0])], [(mean_square, u[2])], [(norm, u[1])], [], [(norm, u[2])], [(mean_square, u[0] + 3)] if u[0] + 3 < TILES else []] if u else []
+            for j, (f, n, c) in enumerate(work):
+                s = f(n, c)
+                if j < len(jobs):
+                    for g, a in jobs[j]:
+                        g(a)
                 empty(*s)

@@ -25,8 +25,10 @@ N_TILE = 512
 ROW_BLOCKS = N_TILE // P
 COLUMN_TILES = D // N_TILE
 CHUNKS = 2 * COLUMN_TILES
+GAIN_ROWS = 4
 
 FLOPS = 2 * H * D * BATCHES * (TOKENS + TOKENS + MEMORY)
+ORDERED_CHUNKS = (2,)
 
 
 def tile_memresprojections_pa_kernel(
@@ -42,8 +44,8 @@ def tile_memresprojections_pa_kernel(
         results = ctx.enter_context(tc.tile_pool(name="results", bufs=14))
         banks = ctx.enter_context(tc.psum_pool(name="banks", bufs=8))
 
-        gain_row = const.tile([P, H], BF16)
-        nc.vector.memset(gain_row[:].bitcast(I32), 0)
+        gain_rows = const.tile([P, H // GAIN_ROWS], BF16)
+        nc.vector.memset(gain_rows[:].bitcast(I32), 0)
 
         token_rows = hidden_states.flatten_outer_dims()
         tokens = {}
@@ -62,7 +64,7 @@ def tile_memresprojections_pa_kernel(
                 nc.sync.dma_start(out=chunk_rows[c][:, j : j + step, :], in_=blocks[:, j : j + step, :])
 
         load_tokens(0)
-        nc.sync.dma_start(out=gain_row[0:1, :], in_=norm_w.unsqueeze(0))
+        nc.sync.dma_start(out=gain_rows[0:GAIN_ROWS, :], in_=norm_w.rearrange("(j c) -> j c", j=GAIN_ROWS))
         load_chunk(0, q_w[0:N_TILE, :], 4)
         load_tokens(1)
         load_chunk(1, q_w[N_TILE:D, :], 2)
@@ -80,19 +82,24 @@ def tile_memresprojections_pa_kernel(
         nc.vector.memset(minus_half[:], -0.5)
         table_warmer = const.tile([P, 1], F32)
         nc.scalar.activation(out=table_warmer[:], in_=minus_half[:], func=ACT.Square)
-        ones = const.tile([P, P], BF16)
-        nc.vector.memset(ones[:], 1.0)
         ident = const.tile([P, P], F32)
         masks.make_identity(nc, ident[:])
 
+        pick = const.tile([P, GAIN_ROWS], BF16)
+        nc.vector.tensor_copy(out=pick[:], in_=ident[:, 0:GAIN_ROWS])
         gain = const.tile([P, HALVES, H // PACK, PAIR], BF16)
+        columns = H // GAIN_ROWS
         words = N_TILE // PACK
         for c in range(H // N_TILE):
             spread = banks.tile([P, N_TILE], F32, tag="bank")
-            nc.tensor.matmul(
-                spread[:], lhsT=ones[:], rhs=gain_row[:, c * N_TILE : (c + 1) * N_TILE],
-                start=True, stop=True,
-            )
+            for i in range(N_TILE // columns):
+                j = c * (N_TILE // columns) + i
+                nc.tensor.matmul(
+                    spread[:, i * columns : (i + 1) * columns],
+                    lhsT=pick[:, j : j + 1].to_broadcast([P, P]),
+                    rhs=gain_rows[:],
+                    start=True, stop=True,
+                )
             nc.vector.tensor_copy(
                 out=gain[:, :, c * words : (c + 1) * words, :],
                 in_=spread[:].rearrange("p (w u e) -> p u w e", u=HALVES, e=PAIR),
@@ -170,20 +177,35 @@ def tile_memresprojections_pa_kernel(
         side_by_side = {}
         chunk_mx = {}
 
+        ordered = {}
+
+        def order_chunk(c, step):
+            ordered[c] = stage.tile(
+                [P, ROW_BLOCKS, HALVES, H // PACK], F32, tag="ordered", name="ordered%d" % c, bufs=2
+            )
+            for j in range(0, ROW_BLOCKS, step):
+                nc.vector.tensor_copy(
+                    out=ordered[c][:, j : j + step, :, :],
+                    in_=chunk_rows[c][:, j : j + step, :].bitcast(F32).rearrange(
+                        "p j (w u) -> p j u w", u=HALVES
+                    ),
+                )
+
         def turn_chunk(c):
             side_by_side[c] = stage.tile(
                 [P, PASSES * N_TILE * PACK], BF16, tag="side", name="side%d" % c, bufs=2, align_bytes=64
             )
             as_pairs = side_by_side[c][:].bitcast(F32).rearrange("p (g r u) -> p g r u", g=PASSES, u=HALVES)
             for j in range(ROW_BLOCKS):
-                pairs = chunk_rows[c][:, j, :].bitcast(F32)
                 bank = banks.tile([P, PASSES, HALVES, P], F32, tag="bank")
                 for g in range(PASSES):
                     for u in range(HALVES):
-                        first = HALVES * P * g + u
-                        nc.tensor.transpose(
-                            bank[:, g, u, :], pairs[:, first : HALVES * P * (g + 1) : HALVES], ident[:]
-                        )
+                        if c in ORDERED_CHUNKS:
+                            in_ = ordered[c][:, j, u, g * P : (g + 1) * P]
+                        else:
+                            first = HALVES * P * g + u
+                            in_ = chunk_rows[c][:, j, :].bitcast(F32)[:, first : HALVES * P * (g + 1) : HALVES]
+                        nc.tensor.transpose(bank[:, g, u, :], in_, ident[:])
                 copy = nc.vector.tensor_copy if j == 0 else nc.scalar.copy
                 copy(
                     out=as_pairs[:, :, j * P : (j + 1) * P, :],
@@ -266,6 +288,7 @@ def tile_memresprojections_pa_kernel(
         mean_square(2)
         sums = products([(0, 0)])
         group(1)
+        order_chunk(2, 2)
         norm(2)
         quantise(1)
         quantise_chunk(1)

@@ -25,10 +25,10 @@ N_TILE = 512
 ROW_BLOCKS = N_TILE // P
 COLUMN_TILES = D // N_TILE
 CHUNKS = 2 * COLUMN_TILES
+SCALAR_ROOTS = 3
 GAIN_ROWS = 4
 
 FLOPS = 2 * H * D * BATCHES * (TOKENS + TOKENS + MEMORY)
-ORDERED_CHUNKS = (2,)
 
 
 def tile_memresprojections_pa_kernel(
@@ -80,8 +80,10 @@ def tile_memresprojections_pa_kernel(
 
         minus_half = const.tile([P, 1], F32)
         nc.vector.memset(minus_half[:], -0.5)
+        eps = const.tile([P, 1], F32)
+        nc.vector.memset(eps[:], EPS)
         table_warmer = const.tile([P, 1], F32)
-        nc.scalar.activation(out=table_warmer[:], in_=minus_half[:], func=ACT.Square)
+        nc.scalar.activation(out=table_warmer[:], in_=minus_half[:], func=ACT.Abs_reciprocal_sqrt)
         ident = const.tile([P, P], F32)
         masks.make_identity(nc, ident[:])
 
@@ -117,11 +119,16 @@ def tile_memresprojections_pa_kernel(
             nc.scalar.activation(
                 out=squares[:], in_=tokens[n][:], func=ACT.Square, scale=H**-0.5, accum_out=mean_sq[:]
             )
+            inv_rms[n] = stage.tile([P, 1], F32, tag="inv_rms", name="inv_rms%d" % n)
+            if n < SCALAR_ROOTS:
+                nc.scalar.activation(
+                    out=inv_rms[n][:], in_=mean_sq[:], func=ACT.Abs_reciprocal_sqrt, bias=eps[:]
+                )
+                return
             shifted = stage.tile([P, 1], F32, tag="shifted")
             nc.gpsimd.tensor_scalar(
                 out=shifted[:], in0=mean_sq[:], scalar1=1.0, scalar2=EPS, op0=ALU.mult, op1=ALU.add
             )
-            inv_rms[n] = stage.tile([P, 1], F32, tag="inv_rms", name="inv_rms%d" % n)
             nc.gpsimd.tensor_tensor(out=inv_rms[n][:], in0=shifted[:], in1=minus_half[:], op=ALU.pow)
 
         def norm(n):
@@ -177,35 +184,20 @@ def tile_memresprojections_pa_kernel(
         side_by_side = {}
         chunk_mx = {}
 
-        ordered = {}
-
-        def order_chunk(c, step):
-            ordered[c] = stage.tile(
-                [P, ROW_BLOCKS, HALVES, H // PACK], F32, tag="ordered", name="ordered%d" % c, bufs=2
-            )
-            for j in range(0, ROW_BLOCKS, step):
-                nc.vector.tensor_copy(
-                    out=ordered[c][:, j : j + step, :, :],
-                    in_=chunk_rows[c][:, j : j + step, :].bitcast(F32).rearrange(
-                        "p j (w u) -> p j u w", u=HALVES
-                    ),
-                )
-
         def turn_chunk(c):
             side_by_side[c] = stage.tile(
                 [P, PASSES * N_TILE * PACK], BF16, tag="side", name="side%d" % c, bufs=2, align_bytes=64
             )
             as_pairs = side_by_side[c][:].bitcast(F32).rearrange("p (g r u) -> p g r u", g=PASSES, u=HALVES)
             for j in range(ROW_BLOCKS):
+                pairs = chunk_rows[c][:, j, :].bitcast(F32)
                 bank = banks.tile([P, PASSES, HALVES, P], F32, tag="bank")
                 for g in range(PASSES):
                     for u in range(HALVES):
-                        if c in ORDERED_CHUNKS:
-                            in_ = ordered[c][:, j, u, g * P : (g + 1) * P]
-                        else:
-                            first = HALVES * P * g + u
-                            in_ = chunk_rows[c][:, j, :].bitcast(F32)[:, first : HALVES * P * (g + 1) : HALVES]
-                        nc.tensor.transpose(bank[:, g, u, :], in_, ident[:])
+                        first = HALVES * P * g + u
+                        nc.tensor.transpose(
+                            bank[:, g, u, :], pairs[:, first : HALVES * P * (g + 1) : HALVES], ident[:]
+                        )
                 copy = nc.vector.tensor_copy if j == 0 else nc.scalar.copy
                 copy(
                     out=as_pairs[:, :, j * P : (j + 1) * P, :],
@@ -288,7 +280,6 @@ def tile_memresprojections_pa_kernel(
         mean_square(2)
         sums = products([(0, 0)])
         group(1)
-        order_chunk(2, 2)
         norm(2)
         quantise(1)
         quantise_chunk(1)

@@ -25,7 +25,6 @@ N_TILE = 512
 ROW_BLOCKS = N_TILE // P
 COLUMN_TILES = D // N_TILE
 CHUNKS = 2 * COLUMN_TILES
-SCALAR_ROOTS = 3
 GAIN_ROWS = 4
 
 FLOPS = 2 * H * D * BATCHES * (TOKENS + TOKENS + MEMORY)
@@ -78,12 +77,10 @@ def tile_memresprojections_pa_kernel(
         for n in range(6, TILES):
             load_tokens(n)
 
-        minus_half = const.tile([P, 1], F32)
-        nc.vector.memset(minus_half[:], -0.5)
         eps = const.tile([P, 1], F32)
         nc.vector.memset(eps[:], EPS)
         table_warmer = const.tile([P, 1], F32)
-        nc.scalar.activation(out=table_warmer[:], in_=minus_half[:], func=ACT.Abs_reciprocal_sqrt)
+        nc.scalar.activation(out=table_warmer[:], in_=eps[:], func=ACT.Abs_reciprocal_sqrt)
         ident = const.tile([P, P], F32)
         masks.make_identity(nc, ident[:])
 
@@ -120,16 +117,9 @@ def tile_memresprojections_pa_kernel(
                 out=squares[:], in_=tokens[n][:], func=ACT.Square, scale=H**-0.5, accum_out=mean_sq[:]
             )
             inv_rms[n] = stage.tile([P, 1], F32, tag="inv_rms", name="inv_rms%d" % n)
-            if n < SCALAR_ROOTS:
-                nc.scalar.activation(
-                    out=inv_rms[n][:], in_=mean_sq[:], func=ACT.Abs_reciprocal_sqrt, bias=eps[:]
-                )
-                return
-            shifted = stage.tile([P, 1], F32, tag="shifted")
-            nc.gpsimd.tensor_scalar(
-                out=shifted[:], in0=mean_sq[:], scalar1=1.0, scalar2=EPS, op0=ALU.mult, op1=ALU.add
+            nc.scalar.activation(
+                out=inv_rms[n][:], in_=mean_sq[:], func=ACT.Abs_reciprocal_sqrt, bias=eps[:]
             )
-            nc.gpsimd.tensor_tensor(out=inv_rms[n][:], in0=shifted[:], in1=minus_half[:], op=ALU.pow)
 
         def norm(n):
             normed[n] = stage.tile([P, HALVES, H // PACK, PAIR], BF16, tag="normed", name="normed%d" % n)
@@ -207,13 +197,11 @@ def tile_memresprojections_pa_kernel(
         def quantise_chunk(c):
             codes = operands.tile([P, PASSES, N_TILE], U32, name="chunk_codes%d" % c, align_bytes=64)
             scales = operands.tile([P, PASSES, N_TILE], U8, name="chunk_scales%d" % c, align_bytes=64)
-            width = N_TILE * PACK
-            for g in range(PASSES):
-                nc.vector.quantize_mx(
-                    out=codes[:, g, :].bitcast(FP8X4),
-                    scales=scales[:, g, :],
-                    in_=side_by_side[c][:, g * width : (g + 1) * width],
-                )
+            nc.vector.quantize_mx(
+                out=codes[:].rearrange("p g r -> p (g r)").bitcast(FP8X4),
+                scales=scales[:].rearrange("p g r -> p (g r)"),
+                in_=side_by_side[c][:],
+            )
             chunk_mx[c] = (codes, scales)
 
         q_out = out_0.flatten_outer_dims()

@@ -146,7 +146,8 @@ def tile_memresprojections_pa_kernel(
             grouped[n] = stage.tile(
                 [P, PASSES * P * PACK], BF16, tag="grouped", name="grouped%s" % str(n), align_bytes=64
             )
-            nc.scalar.copy(
+            copy = nc.vector.tensor_copy if isinstance(n, tuple) else nc.scalar.copy
+            copy(
                 out=grouped[n][:].bitcast(F32).rearrange("p (g r u) -> p g r u", g=PASSES, u=HALVES),
                 in_=turned[n][:].rearrange("p g u r -> p g r u"),
             )
@@ -244,9 +245,6 @@ def tile_memresprojections_pa_kernel(
             bank = multiply(pool_mx[("m", b)], slice(0, P), c)
             return bank, ("m", b), out_1[b, TOKENS : TOKENS + MEMORY, :], c
 
-        def became_possible(w):
-            return [(n, c) for c in range(w + 1) for n in range(w + 1) if max(n, c) == w]
-
         def products(pairs):
             return [token_product(n, c) for n, c in pairs]
 
@@ -258,42 +256,44 @@ def tile_memresprojections_pa_kernel(
         norm(0)
         turn_chunk(0)
         turn(0)
-        mean_square(1)
         group(0)
-        turn_chunk(1)
-        norm(1)
-        turn(1)
+        mean_square(1)
         quantise_chunk(0)
+        turn_chunk(1)
         quantise(0)
+        norm(1)
         mean_square(2)
         sums = products([(0, 0)])
-        group(1)
-        norm(2)
-        quantise(1)
         quantise_chunk(1)
+        turn(1)
+        group(1)
         empty_all(sums)
-        mean_square(3)
+        quantise(1)
         turn_chunk(2)
-        turn(2)
+        norm(2)
         sums = products([(1, 0), (0, 1), (1, 1)])
-        norm(3)
-        group(2)
+        mean_square(3)
         quantise_chunk(2)
-        quantise(2)
-        empty_all(sums)
-        mean_square(4)
+        turn(2)
+        empty_all(sums[:1])
+        group(2)
+        empty_all(sums[1:])
         turn_chunk(3)
+        quantise(2)
         turn_memory(0)
-        mean_square(5)
-        norm(4)
+        norm(3)
+        mean_square(4)
         quantise_chunk(3)
+        sums = products([(0, 2), (1, 2), (2, 0), (2, 1), (2, 2)])
         group(("m", 0))
-        sums = products([(2, 0), (2, 1), (0, 2), (1, 2), (2, 2)])
+        mean_square(5)
         empty_all(sums[:2])
-        norm(5)
+        norm(4)
+        empty_all(sums[2:4])
         quantise(("m", 0))
-        empty_all(sums[2:])
+        empty_all(sums[4:])
         sums = products([(0, 3), (1, 3), (2, 3)])
+        norm(5)
         empty_all(sums)
         mean_square(6)
         for b in range(1, BATCHES):
@@ -311,7 +311,7 @@ def tile_memresprojections_pa_kernel(
                 work += [(token_product, n, c) for c in range(CHUNKS)]
             if b == BATCHES - 1:
                 work[-CHUNKS:-CHUNKS] = [(memory_product, b, 2), (memory_product, b, 3)]
-            jobs = [[(quantise, t[1]), (group, t[2])], [(quantise, t[2]), (group, m)], [(quantise, m)]]
+            jobs = [[(quantise, t[1]), (group, t[2]), (group, m)], [(quantise, t[2])], [(quantise, m)]]
             jobs += [[(mean_square, u[1])], [(norm, u[0])], [(mean_square, u[2])], [(norm, u[1])], [], [(norm, u[2])], [(mean_square, u[0] + 3)] if u[0] + 3 < TILES else []] if u else []
             for j, (f, n, c) in enumerate(work):
                 s = f(n, c)

from contextlib import ExitStack

import concourse.masks as masks
import concourse.mybir as mybir

F32 = mybir.dt.float32
BF16 = mybir.dt.bfloat16
I32 = mybir.dt.int32
U32 = mybir.dt.uint32
U8 = mybir.dt.uint8
FP8X4 = mybir.dt.float8_e4m3fn_x4
ACT = mybir.ActivationFunctionType
ALU = mybir.AluOpType

P = 128
PACK = 4
PAIR = 2
BATCHES, TOKENS, MEMORY, H, D = 4, 384, 128, 1024, 1024
EPS = 1e-6
PASSES = H // (P * PACK)
HALVES = PACK // PAIR
BATCH_TILES = TOKENS // P
TILES = BATCHES * BATCH_TILES
N_TILE = 512
ROW_BLOCKS = N_TILE // P
COLUMN_TILES = D // N_TILE
CHUNKS = 2 * COLUMN_TILES
GAIN_ROWS = 4

FLOPS = 2 * H * D * BATCHES * (TOKENS + TOKENS + MEMORY)


def tile_memresprojections_pa_kernel(
    tc, hidden_states, memory_state, q_w, k_w, norm_w, out_0, out_1
):
    nc = tc.nc
    with ExitStack() as ctx:
        ctx.enter_context(tc.manual_schedule())
        const = ctx.enter_context(tc.tile_pool(name="const", bufs=1))
        inputs = ctx.enter_context(tc.tile_pool(name="inputs", bufs=1))
        operands = ctx.enter_context(tc.tile_pool(name="operands", bufs=1))
        stage = ctx.enter_context(tc.tile_pool(name="stage", bufs=4))
        results = ctx.enter_context(tc.tile_pool(name="results", bufs=14))
        banks = ctx.enter_context(tc.psum_pool(name="banks", bufs=8))

        gain_rows = const.tile([P, H // GAIN_ROWS], BF16)
        nc.vector.memset(gain_rows[:].bitcast(I32), 0)

        token_rows = hidden_states.flatten_outer_dims()
        tokens = {}

        def load_tokens(n):
            tokens[n] = inputs.tile([P, H], BF16, name="tokens%d" % n)
            nc.sync.dma_start(out=tokens[n][:], in_=token_rows[n * P : (n + 1) * P, :])

        chunk_rows = {}

        def load_chunk(c, source, pieces):
            chunk_rows[c] = inputs.tile([P, ROW_BLOCKS, H], BF16, name="rows%d" % c)
            blocks = source.rearrange("(j p) h -> p j h", p=P)
            step = ROW_BLOCKS // pieces
            for j in range(0, ROW_BLOCKS, step):
                nc.sync.dma_start(out=chunk_rows[c][:, j : j + step, :], in_=blocks[:, j : j + step, :])

        load_tokens(0)
        nc.sync.dma_start(out=gain_rows[0:GAIN_ROWS, :], in_=norm_w.rearrange("(j c) -> j c", j=GAIN_ROWS))
        load_chunk(0, q_w[0:N_TILE, :], 4)
        load_tokens(1)
        load_chunk(1, q_w[N_TILE:D, :], 2)
        load_tokens(2)
        load_chunk(2, k_w[0:N_TILE, :], 2)
        load_tokens(3)
        load_chunk(3, k_w[N_TILE:D, :], 2)
        load_tokens(4)
        load_tokens(5)
        load_chunk(CHUNKS, memory_state.flatten_outer_dims(), 2)
        for n in range(6, TILES):
            load_tokens(n)

        eps = const.tile([P, 1], F32)
        nc.vector.memset(eps[:], EPS)
        table_warmer = const.tile([P, 1], F32)
        nc.scalar.activation(out=table_warmer[:], in_=eps[:], func=ACT.Abs_reciprocal_sqrt)
        ident = const.tile([P, P], F32)
        masks.make_identity(nc, ident[:])

        pick = const.tile([P, GAIN_ROWS], BF16)
        nc.vector.tensor_copy(out=pick[:], in_=ident[:, 0:GAIN_ROWS])
        gain = const.tile([P, HALVES, H // PACK, PAIR], BF16)
        columns = H // GAIN_ROWS
        words = N_TILE // PACK
        for c in range(H // N_TILE):
            spread = banks.tile([P, N_TILE], F32, tag="bank")
            for i in range(N_TILE // columns):
                j = c * (N_TILE // columns) + i
                nc.tensor.matmul(
                    spread[:, i * columns : (i + 1) * columns],
                    lhsT=pick[:, j : j + 1].to_broadcast([P, P]),
                    rhs=gain_rows[:],
                    start=True, stop=True,
                )
            nc.vector.tensor_copy(
                out=gain[:, :, c * words : (c + 1) * words, :],
                in_=spread[:].rearrange("p (w u e) -> p u w e", u=HALVES, e=PAIR),
            )

        inv_rms = {}
        normed = {}
        turned = {}
        grouped = {}
        pool_mx = {}

        def mean_square(n):
            squares = stage.tile([P, H], BF16, tag="squares", bufs=2)
            mean_sq = stage.tile([P, 1], F32, tag="mean_sq")
            nc.scalar.activation(
                out=squares[:], in_=tokens[n][:], func=ACT.Square, scale=H**-0.5, accum_out=mean_sq[:]
            )
            inv_rms[n] = stage.tile([P, 1], F32, tag="inv_rms", name="inv_rms%d" % n)
            nc.scalar.activation(
                out=inv_rms[n][:], in_=mean_sq[:], func=ACT.Abs_reciprocal_sqrt, bias=eps[:]
            )

        def norm(n):
            normed[n] = stage.tile([P, HALVES, H // PACK, PAIR], BF16, tag="normed", name="normed%d" % n)
            by_half = tokens[n][:].rearrange("p (w u e) -> p u w e", u=HALVES, e=PAIR)
            for u in range(HALVES):
                nc.vector.scalar_tensor_tensor(
                    out=normed[n][:, u, :, :],
                    in0=by_half[:, u, :, :],
                    scalar=inv_rms[n][:],
                    in1=gain[:, u, :, :],
                    op0=ALU.mult,
                    op1=ALU.mult,
                )

        def turn(n):
            turned[n] = banks.tile([P, PASSES, HALVES, P], F32, tag="bank", name="turned%d" % n)
            pairs = normed[n][:].rearrange("p u w e -> p (u w e)").bitcast(F32)
            for g in range(PASSES):
                for u in range(HALVES):
                    first = (PASSES * u + g) * P
                    nc.tensor.transpose(turned[n][:, g, u, :], pairs[:, first : first + P], ident[:])

        def group(n):
            grouped[n] = stage.tile(
                [P, PASSES * P * PACK], BF16, tag="grouped", name="grouped%s" % str(n), align_bytes=64
            )
            copy = nc.vector.tensor_copy if isinstance(n, tuple) else nc.scalar.copy
            copy(
                out=grouped[n][:].bitcast(F32).rearrange("p (g r u) -> p g r u", g=PASSES, u=HALVES),
                in_=turned[n][:].rearrange("p g u r -> p g r u"),
            )

        def quantise(n):
            codes = operands.tile([P, PASSES, P], U32, name="codes%s" % str(n), align_bytes=64)
            scales = operands.tile([P, PASSES, P], U8, name="scales%s" % str(n), align_bytes=64)
            nc.vector.quantize_mx(
                out=codes[:].rearrange("p g r -> p (g r)").bitcast(FP8X4),
                scales=scales[:].rearrange("p g r -> p (g r)"),
                in_=grouped[n][:],
            )
            pool_mx[n] = (codes, scales)


        def turn_memory(b):
            key = ("m", b)
            turned[key] = banks.tile([P, PASSES, HALVES, P], F32, tag="bank", name="mturned%d" % b)
            pairs = chunk_rows[CHUNKS][:, b, :].bitcast(F32)
            for g in range(PASSES):
                for u in range(HALVES):
                    first = HALVES * P * g + u
                    nc.tensor.transpose(turned[key][:, g, u, :], pairs[:, first : HALVES * P * (g + 1) : HALVES], ident[:])

        side_by_side = {}
        chunk_mx = {}

        def turn_chunk(c):
            side_by_side[c] = stage.tile(
                [P, PASSES * N_TILE * PACK], BF16, tag="side", name="side%d" % c, bufs=2, align_bytes=64
            )
            as_pairs = side_by_side[c][:].bitcast(F32).rearrange("p (g r u) -> p g r u", g=PASSES, u=HALVES)
            for j in range(ROW_BLOCKS):
                pairs = chunk_rows[c][:, j, :].bitcast(F32)
                bank = banks.tile([P, PASSES, HALVES, P], F32, tag="bank")
                for g in range(PASSES):
                    for u in range(HALVES):
                        first = HALVES * P * g + u
                        nc.tensor.transpose(
                            bank[:, g, u, :], pairs[:, first : HALVES * P * (g + 1) : HALVES], ident[:]
                        )
                copy = nc.vector.tensor_copy if j == 0 else nc.scalar.copy
                copy(
                    out=as_pairs[:, :, j * P : (j + 1) * P, :],
                    in_=bank[:].rearrange("p g u r -> p g r u"),
                )

        def quantise_chunk(c):
            codes = operands.tile([P, PASSES, N_TILE], U32, name="chunk_codes%d" % c, align_bytes=64)
            scales = operands.tile([P, PASSES, N_TILE], U8, name="chunk_scales%d" % c, align_bytes=64)
            nc.vector.quantize_mx(
                out=codes[:].rearrange("p g r -> p (g r)").bitcast(FP8X4),
                scales=scales[:].rearrange("p g r -> p (g r)"),
                in_=side_by_side[c][:],
            )
            chunk_mx[c] = (codes, scales)

        q_out = out_0.flatten_outer_dims()
        result_tiles = {}

        def multiply(token_mx, token_columns, c):
            token_codes, token_scales = token_mx
            chunk_codes, chunk_scales = chunk_mx[c]
            bank = banks.tile([P, N_TILE], F32, tag="bank")
            for g in range(PASSES):
                nc.tensor.matmul_mx(
                    out=bank[:],
                    lhsT=token_codes[:, g, token_columns].bitcast(FP8X4),
                    lhsT_scale=token_scales[:, g, token_columns],
                    rhs=chunk_codes[:, g, :].bitcast(FP8X4),
                    rhs_scale=chunk_scales[:, g, :],
                    start=(g == 0),
                    stop=(g == PASSES - 1),
                )
            return bank

        def empty(bank, key, out_rows, c):
            column = c % COLUMN_TILES
            if column == 0:
                result_tiles[key] = results.tile([P, D], F32, tag="result", name="result_%s%d" % key)
            result = result_tiles[key]
            copy = nc.scalar.copy if column == 0 else nc.vector.tensor_copy
            copy(out=result[:, column * N_TILE : (column + 1) * N_TILE], in_=bank[:])
            if column == COLUMN_TILES - 1:
                nc.sync.dma_start(out=out_rows, in_=result[:])

        def token_product(n, c):
            b, i = divmod(n, BATCH_TILES)
            bank = multiply(pool_mx[n], slice(0, P), c)
            if c < COLUMN_TILES:
                return bank, ("q", n), q_out[n * P : (n + 1) * P, :], c
            return bank, ("k", n), out_1[b, i * P : (i + 1) * P, :], c

        def memory_product(b, c):
            bank = multiply(pool_mx[("m", b)], slice(0, P), c)
            return bank, ("m", b), out_1[b, TOKENS : TOKENS + MEMORY, :], c

        def products(pairs):
            return [token_product(n, c) for n, c in pairs]

        def empty_all(sums):
            for s in sums:
                empty(*s)

        mean_square(0)
        norm(0)
        turn_chunk(0)
        turn(0)
        group(0)
        mean_square(1)
        quantise_chunk(0)
        turn_chunk(1)
        quantise(0)
        norm(1)
        mean_square(2)
        sums = products([(0, 0)])
        quantise_chunk(1)
        turn(1)
        group(1)
        empty_all(sums)
        quantise(1)
        turn_chunk(2)
        norm(2)
        sums = products([(1, 0), (0, 1), (1, 1)])
        mean_square(3)
        quantise_chunk(2)
        turn(2)
        empty_all(sums[:1])
        group(2)
        empty_all(sums[1:])
        turn_chunk(3)
        quantise(2)
        turn_memory(0)
        norm(3)
        mean_square(4)
        quantise_chunk(3)
        sums = products([(0, 2), (1, 2), (2, 0), (2, 1), (2, 2)])
        group(("m", 0))
        mean_square(5)
        empty_all(sums[:2])
        norm(4)
        empty_all(sums[2:4])
        quantise(("m", 0))
        empty_all(sums[4:])
        sums = products([(0, 3), (1, 3), (2, 3)])
        norm(5)
        empty_all(sums)
        mean_square(6)
        for b in range(1, BATCHES):
            t = [BATCH_TILES * b + i for i in range(BATCH_TILES)]
            m = ("m", b)
            u = [n + BATCH_TILES for n in t if n + BATCH_TILES < TILES]
            for n in t:
                turn(n)
            turn_memory(b)
            group(t[0])
            quantise(t[0])
            group(t[1])
            work = [(memory_product, b - 1, 2), (memory_product, b - 1, 3)]
            for n in t:
                work += [(token_product, n, c) for c in range(CHUNKS)]
            if b == BATCHES - 1:
                work[-CHUNKS:-CHUNKS] = [(memory_product, b, 2), (memory_product, b, 3)]
            jobs = [[(quantise, t[1]), (group, t[2]), (group, m)], [(quantise, t[2])], [(quantise, m)]]
            jobs += [[(mean_square, u[1])], [(norm, u[0])], [(mean_square, u[2])], [(norm, u[1])], [], [(norm, u[2])], [(mean_square, u[0] + 3)] if u[0] + 3 < TILES else []] if u else []
            for j, (f, n, c) in enumerate(work):
                s = f(n, c)
                if j < len(jobs):
                    for g, a in jobs[j]:
                        g(a)
                empty(*s)
